import numpy as np
import ml_dtypes


def mxq(x, axis, fmt="e4m3"):
    dtype, down = {"e4m3": (ml_dtypes.float8_e4m3fn, 7), "e5m2": (ml_dtypes.float8_e5m2, 14)}[fmt]
    v = np.moveaxis(np.asarray(x, np.float32).astype(ml_dtypes.bfloat16).astype(np.float64), axis, -1)
    blocks = v.reshape(v.shape[:-1] + (-1, 32))
    amax = np.abs(blocks).max(-1, keepdims=True)
    byte = np.maximum(np.where(amax > 0, np.frexp(amax)[1] - 1 + 127, 0) - down, 1)
    scale = np.exp2(byte - 127.0)
    codes = (blocks / scale).astype(np.float32).astype(dtype).astype(np.float64)
    return np.moveaxis((codes * scale).reshape(v.shape), -1, axis)


WIDE = False


def mx_kscale(k):
    if not WIDE:
        return np.ones(k)
    levels = np.array([10, -10, 5, -5, 0])
    if k % 512:
        return np.exp2(np.random.permutation(np.resize(levels, k // 32))).repeat(32)
    a = np.empty((k // 512, 16))
    for p in range(k // 512):
        a[p, :8] = np.random.permutation(np.resize(levels, 8))
        for g in range(8):
            far = levels[np.abs(levels - a[p, g]) >= 10]
            a[p, g + 8] = far[np.random.randint(len(far))]
    return np.exp2(a.ravel()).repeat(32)


BF16 = ml_dtypes.bfloat16


def bf(x):
    return np.asarray(x, np.float32).astype(BF16)


def f64(x):
    return np.asarray(x).astype(np.float64)


N, C, E, T, H, CK = 3, 512, 512, 1024, 8, 64
EPS = 1e-5


def setup_inputs():
    s = mx_kscale(N * T)
    u = mx_kscale(E)
    h0 = bf(np.random.standard_normal((N, T, C)) * 0.4)
    x = bf(np.random.standard_normal((N, E, T)))
    m0 = bf(np.random.uniform(0.2, 1.0, (N, 1, T)))
    w0 = bf(np.random.standard_normal((E, C)) * 2.0 / np.sqrt(C))
    bo = bf(np.random.standard_normal(E) * 0.5)
    g = bf(np.random.standard_normal((N, E, T)) * np.exp2(np.random.randint(-6, 1, (N, 1, T))) * 2.0 * u[None, :, None])
    o = f64(h0) @ f64(w0).T + f64(bo)
    y = o.transpose(0, 2, 1) * f64(m0) + f64(x)
    mean = y.mean(-1, keepdims=True)
    rstd = 1.0 / np.sqrt(np.square(y - mean).mean(-1, keepdims=True) + EPS)
    return {
        "h_attn": bf(f64(h0) * s.reshape(N, T, 1)),
        "x": x,
        "masks": bf(f64(m0) / s.reshape(N, 1, T)),
        "Wo": bf(f64(w0) / u[:, None]),
        "bo": bo,
        "y": np.asarray(y, np.float32),
        "mean": np.asarray(mean, np.float32),
        "rstd": np.asarray(rstd, np.float32),
        "grad_out": g,
    }


def reference(h_attn, x, masks, Wo, bo, y, mean, rstd, grad_out):
    g = f64(grad_out)
    r = f64(rstd)
    yhat = (f64(y) - f64(mean)) * r
    g_mean = g.mean(-1, keepdims=True)
    gy_mean = (g * yhat).mean(-1, keepdims=True)
    dy = r * (g - g_mean - yhat * gy_mean)
    dz = (dy * f64(masks)).transpose(0, 2, 1).reshape(N * T, E)
    dh = mxq(dz, 1, "e5m2") @ mxq(f64(Wo), 0, "e4m3")
    dw = mxq(dz, 0, "e5m2").T @ mxq(f64(h_attn).reshape(N * T, C), 0, "e4m3")
    return dh.reshape(N, T, C), dw

@@ -1,0 +1,314 @@
+from contextlib import ExitStack
+
+import concourse.mybir as mybir
+from concourse.masks import make_identity
+
+F32 = mybir.dt.float32
+BF16 = mybir.dt.bfloat16
+U32 = mybir.dt.uint32
+U8 = mybir.dt.uint8
+E4M3 = mybir.dt.float8_e4m3fn_x4
+E5M2 = mybir.dt.float8_e5m2_x4
+ALU = mybir.AluOpType
+ACT = mybir.ActivationFunctionType
+
+N, T, C, E = 3, 1024, 512, 512
+P = 128
+PACK = 4
+KP = P * PACK
+PASSES = N * T // KP
+STEPS = PASSES * PACK
+RUN = 8
+FLOPS = 2 * 2 * N * T * C * E
+BYTES = N * T * C * 2 + N * T * 2 + E * C * 2 + N * E * T * 4 + 2 * N * E * 4 + N * E * T * 2 + N * T * C * 4 + E * C * 4
+
+
+def tile_transformerencoderblock_pa_v_kernel(tc, h_attn, x, masks, Wo, bo, y, mean, rstd, grad_out, out_0, out_1):
+    nc = tc.nc
+    with ExitStack() as ctx:
+        const = ctx.enter_context(tc.tile_pool(name="const", bufs=1))
+        work = ctx.enter_context(tc.tile_pool(name="work", bufs=2))
+        psum = ctx.enter_context(tc.psum_pool(name="psum", bufs=1))
+        ctx.enter_context(tc.manual_schedule())
+
+        g_hbm = grad_out.rearrange("n (p j) t -> n j p t", j=PACK)
+        y_hbm = y.rearrange("n (p j) t -> n j p t", j=PACK)
+        h_hbm = h_attn.rearrange("n (g q s i) c -> n g s q i c", g=2, s=PACK, i=RUN)
+        o0_hbm = out_0.rearrange("n (g q s i) c -> n g s q i c", g=2, s=PACK, i=RUN)
+        o1_hbm = out_1.rearrange("(a m u e) c -> u a m e c", a=2, u=2, e=2)
+
+        g_sb, y_sb, h_sb = {}, {}, {}
+        rg, uu, s_gy, s_rg, coef, shift = {}, {}, {}, {}, {}, {}
+        dz_rows, chan, chan_q, tok_q, h_q, acc0 = {}, {}, {}, {}, {}, {}
+        grouped = {}
+
+        def load_unit(n, j):
+            g_sb[n, j] = work.tile([P, T], BF16, name="g_sb", bufs=8, align_bytes=256)
+            nc.sync.dma_start(out=g_sb[n, j][:], in_=g_hbm[n, j])
+            y_sb[n, j] = work.tile([P, T], F32, name="y_sb", bufs=8, align_bytes=256)
+            nc.sync.dma_start(out=y_sb[n, j][:], in_=y_hbm[n, j])
+
+        def load_h(ps):
+            h_sb[ps] = work.tile([P, PACK * C], BF16, name="h_sb", bufs=3, align_bytes=256)
+            for s in range(PACK):
+                nc.sync.dma_start(out=h_sb[ps][:, s * C:(s + 1) * C], in_=h_hbm[ps // 2, ps % 2, s])
+
+        def by_slot(ap):
+            return ap.rearrange("p (a s i) -> p s a i", s=PACK, i=RUN)
+
+        def slot_major(ap):
+            return ap.rearrange("p (s a i) -> p s a i", s=PACK, i=RUN)
+
+        load_unit(0, 0)
+        mean_sb = const.tile([P, N, PACK], F32, name="mean_sb")
+        nc.sync.dma_start(out=mean_sb[:], in_=mean.rearrange("n (p j) o -> p n (j o)", j=PACK))
+        rstd_sb = const.tile([P, N, PACK], F32, name="rstd_sb")
+        nc.sync.dma_start(out=rstd_sb[:], in_=rstd.rearrange("n (p j) o -> p n (j o)", j=PACK))
+        load_unit(0, 1)
+        mask_rows = const.tile([PASSES, KP], BF16, name="mask_rows")
+        nc.sync.dma_start(out=mask_rows[:], in_=masks.rearrange("n o (g t) -> (n o g) t", g=2))
+        load_unit(0, 2)
+        load_unit(0, 3)
+        load_unit(1, 0)
+        w_sb = work.tile([P, PACK * C], BF16, name="h_sb", bufs=3, align_bytes=256)
+        nc.sync.dma_start(out=w_sb[:], in_=Wo.rearrange("(p j) c -> p (j c)", j=PACK))
+        load_unit(1, 1)
+        load_h(0)
+        load_unit(1, 2)
+        load_unit(1, 3)
+        load_h(1)
+
+        ident = const.tile([P, P], F32, name="ident")
+        make_identity(nc, ident[:])
+        mask_pad = const.tile([P, KP], F32, name="mask_pad")
+        nc.gpsimd.memset(mask_pad[:], 0.0)
+
+        r2 = const.tile([P, N * PACK], F32, name="r2")
+        kk = const.tile([P, N * PACK, 2], F32, name="kk")
+        rs = rstd_sb[:].rearrange("p n j -> p (n j)")
+        mn = mean_sb[:].rearrange("p n j -> p (n j)")
+        nc.vector.tensor_tensor(out=r2[:], in0=rs, in1=rs, op=ALU.mult)
+        nc.vector.scalar_tensor_tensor(out=kk[:, :, 0], in0=r2[:], scalar=-1.0 / T, in1=rs, op0=ALU.mult, op1=ALU.mult)
+        nc.vector.tensor_tensor(out=kk[:, :, 1], in0=kk[:, :, 0], in1=mn, op=ALU.mult)
+
+        def scale_g(n, j):
+            rg[n, j] = work.tile([P, T], F32, name="rg", bufs=8)
+            s_rg[n, j] = work.tile([P, 1], F32, name="s_rg", bufs=4)
+            nc.scalar.activation(out=slot_major(rg[n, j][:]), in_=by_slot(g_sb[n, j][:]), func=ACT.Copy,
+                                 scale=rstd_sb[:, n, j:j + 1], accum_out=s_rg[n, j][:])
+
+        def stats(n, j):
+            prod = work.tile([P, T], F32, name="prod", bufs=1)
+            s_gy[n, j] = work.tile([P, 1], F32, name="s_gy", bufs=4)
+            nc.vector.scalar_tensor_tensor(out=prod[:], in0=y_sb[n, j][:], scalar=mean_sb[:, n, j:j + 1], in1=g_sb[n, j][:],
+                                           op0=ALU.subtract, op1=ALU.mult, accum_out=s_gy[n, j][:])
+
+        def slope(n, j):
+            coef[n, j] = work.tile([P, 2], F32, name="coef", bufs=4)
+            nc.vector.tensor_scalar(out=coef[n, j][:], in0=kk[:, n * PACK + j, :], scalar1=s_gy[n, j][:], scalar2=None, op0=ALU.mult)
+
+        def offset(n, j):
+            shift[n, j] = work.tile([P, 1], F32, name="shift", bufs=4)
+            nc.vector.scalar_tensor_tensor(out=shift[n, j][:], in0=s_rg[n, j][:], scalar=-1.0 / T, in1=coef[n, j][:, 1:2],
+                                           op0=ALU.mult, op1=ALU.subtract)
+
+        def scale_y(n, j):
+            uu[n, j] = work.tile([P, T], F32, name="uu", bufs=8)
+            nc.vector.tensor_scalar(out=slot_major(uu[n, j][:]), in0=by_slot(y_sb[n, j][:]), scalar1=coef[n, j][:, 0:1],
+                                    scalar2=shift[n, j][:], op0=ALU.mult, op1=ALU.add)
+
+        def interleave(key, src):
+            grouped[key] = work.tile([P, PACK * C], BF16, name="grouped", bufs=2, align_bytes=64)
+            nc.vector.tensor_copy(out=grouped[key][:].rearrange("p (c i s) -> p c s i", s=PACK, i=4),
+                                  in_=src[:].rearrange("p (s c i) -> p c s i", s=PACK, i=4))
+
+        def quantize(key, name, fmt, bufs):
+            codes = work.tile([P, C], U32, name=name + "_codes", bufs=bufs, align_bytes=64)
+            scales = work.tile([P, C], U8, name=name + "_scales", bufs=bufs, align_bytes=64)
+            nc.vector.quantize_mx(out=codes[:].bitcast(fmt), scales=scales[:], in_=grouped[key][:])
+            return codes, scales
+
+        scale_g(0, 0)
+        stats(0, 0)
+        nc.scalar.copy(out=mask_pad[0:PASSES, :].rearrange("p (s q i) -> p s q i", s=PACK, i=RUN),
+                       in_=mask_rows[:].rearrange("p (q s i) -> p s q i", s=PACK, i=RUN))
+        slope(0, 0)
+        offset(0, 0)
+        mask_ps = psum.tile([P, PACK, P], F32, name="dy_ps", bufs=2)
+        for s in range(PACK):
+            nc.tensor.transpose(mask_ps[:, s, :], mask_pad[:, s * P:(s + 1) * P], ident[:])
+        for j in range(1, PACK):
+            scale_g(0, j)
+            stats(0, j)
+            slope(0, j)
+            scale_y(0, j - 1)
+            offset(0, j)
+        mask_col = const.tile([P, PACK, PASSES], F32, name="mask_col")
+        nc.scalar.copy(out=mask_col[:], in_=mask_ps[:, :, 0:PASSES])
+        scale_y(0, PACK - 1)
+        for j in range(PACK):
+            load_unit(2, j)
+        scale_g(1, 0)
+        stats(1, 0)
+        slope(1, 0)
+
+        acc1 = [psum.tile([P, C], F32, name="acc1_%d" % k) for k in range(PACK)]
+        w_q = []
+
+        def turn_dy(step):
+            ps, s = divmod(step, PACK)
+            n, half = divmod(ps, 2)
+            bank = psum.tile([P, PACK, P], F32, name="dy_ps", bufs=2)
+            cols = slice(s * 2 * P + half * P, s * 2 * P + (half + 1) * P)
+            for j in range(PACK):
+                nc.tensor.matmul(bank[:, j, :], lhsT=rg[n, j][:, cols], rhs=ident[:], start=True, stop=False, is_transpose=True)
+                nc.tensor.matmul(bank[:, j, :], lhsT=uu[n, j][:, cols], rhs=ident[:], start=False, stop=True, is_transpose=True)
+            return bank
+
+        def round_dz(step, bank):
+            ps, s = divmod(step, PACK)
+            if s == 0:
+                dz_rows[ps] = work.tile([P, PACK * E], BF16, name="dz_rows", bufs=2, align_bytes=64)
+            nc.scalar.activation(out=dz_rows[ps][:, s * E:(s + 1) * E].rearrange("p (u m e) -> p u m e", u=2, e=2),
+                                 in_=bank[:].rearrange("p (u e) m -> p u m e", u=2), func=ACT.Copy,
+                                 scale=mask_col[:, s, ps:ps + 1])
+
+        def turn_dz(step):
+            ps, s = divmod(step, PACK)
+            words = dz_rows[ps][:, s * E:(s + 1) * E].bitcast(F32)
+            bank = psum.tile([P, 2, P], F32, name="dz_ps")
+            for u in range(2):
+                nc.tensor.transpose(bank[:, u, :], words[:, u * P:(u + 1) * P], ident[:])
+            chan[step] = work.tile([P, E], BF16, name="chan", bufs=3, align_bytes=64)
+            nc.scalar.copy(out=chan[step][:].bitcast(F32).rearrange("p (t u) -> p t u", u=2), in_=bank[:].rearrange("p u t -> p t u"))
+
+        def quantize_chan(step):
+            codes = work.tile([P, P], U32, name="chan_codes", bufs=3, align_bytes=64)
+            scales = work.tile([P, P], U8, name="chan_scales", bufs=3, align_bytes=64)
+            nc.vector.quantize_mx(out=codes[:].bitcast(E5M2), scales=scales[:], in_=chan[step][:])
+            chan_q[step] = (codes, scales)
+
+        def mult_out0(step, name="acc0", bufs=1):
+            codes, scales = chan_q[step]
+            acc0[step] = psum.tile([P, C], F32, name=name, bufs=bufs)
+            nc.tensor.matmul_mx(out=acc0[step][:], lhsT=codes[:].bitcast(E5M2), lhsT_scale=scales[:],
+                                rhs=w_q[0][:].bitcast(E4M3), rhs_scale=w_q[1][:], start=True, stop=True)
+
+        def mult_out1(ps, k, codes, scales):
+            nc.tensor.matmul_mx(out=acc1[k][:], lhsT=codes.bitcast(E5M2), lhsT_scale=scales,
+                                rhs=h_q[ps][0][:].bitcast(E4M3), rhs_scale=h_q[ps][1][:], start=(ps == 0), stop=(ps == PASSES - 1))
+
+        def mult_out1_tile(ps, k):
+            codes, scales = tok_q[ps]
+            mult_out1(ps, k, codes[:, k * P:(k + 1) * P], scales[:, k * P:(k + 1) * P])
+
+        def store(dst, acc, on_vector):
+            res = work.tile([P, C], F32, name="res", bufs=8, align_bytes=256)
+            if on_vector:
+                nc.vector.tensor_copy(out=res[:], in_=acc[:])
+            else:
+                nc.scalar.copy(out=res[:], in_=acc[:])
+            nc.sync.dma_start(out=dst, in_=res[:])
+
+        def store_out0(step, on_vector):
+            ps, s = divmod(step, PACK)
+            store(o0_hbm[ps // 2, ps % 2, s], acc0[step], on_vector)
+
+        for step in range(STEPS):
+            ps, s = divmod(step, PACK)
+            nxt = (step + 1) // (2 * PACK) + 1
+            j = ((step + 1) % (2 * PACK)) // 2
+            last_phase = step >= STEPS - 2 * PACK
+            if step >= 4 and not (last_phase and step % 2 == 1):
+                store_out0(step - 4, False)
+            bank = turn_dy(step)
+            if step % 2 == 1 and nxt < N:
+                scale_g(nxt, j)
+            round_dz(step, bank)
+            if step >= 1:
+                turn_dz(step - 1)
+            if step >= 4 and last_phase and step % 2 == 1:
+                store_out0(step - 4, True)
+            if step >= 2:
+                quantize_chan(step - 2)
+            if nxt < N:
+                if step % 2 == 1:
+                    stats(nxt, j)
+                else:
+                    offset(nxt, j)
+            if s == 0:
+                if ps == 0:
+                    interleave("w", w_sb)
+                else:
+                    interleave(("dz", ps - 1), dz_rows[ps - 1])
+            elif s == 1:
+                if ps == 0:
+                    w_q.extend(quantize("w", "w", E4M3, 1))
+                else:
+                    tok_q[ps - 1] = quantize(("dz", ps - 1), "tok", E5M2, 2)
+            elif s == 2:
+                interleave(("h", ps), h_sb[ps])
+                if ps + 2 < PASSES:
+                    load_h(ps + 2)
+            else:
+                h_q[ps] = quantize(("h", ps), "h", E4M3, 2)
+            if nxt < N:
+                if step % 2 == 1:
+                    slope(nxt, j)
+                else:
+                    scale_y(nxt, j)
+            if step >= 3:
+                mult_out0(step - 3)
+            if step >= 6 and step < STEPS - 2:
+                mult_out1_tile((step - 6) // PACK, (step - 6) % PACK)
+            elif step >= STEPS - 2:
+                for k in range(2):
+                    mult_out1_tile(PASSES - 2, 2 * (step - STEPS + 2) + k)
+
+        last = PASSES - 1
+        tail_in = {}
+        tail_q = {}
+
+        def tail_interleave(k):
+            tail_in[k] = work.tile([P, PACK * P], BF16, name="chan", bufs=3, align_bytes=64)
+            nc.vector.tensor_copy(out=tail_in[k][:].rearrange("p (c i s) -> p c s i", s=PACK, i=4),
+                                  in_=dz_rows[last][:].rearrange("p (s c i) -> p c s i", s=PACK, i=4)[:, k * 32:(k + 1) * 32])
+
+        def tail_quantize(k):
+            codes = work.tile([P, P], U32, name="tail_codes", bufs=4, align_bytes=64)
+            scales = work.tile([P, P], U8, name="tail_scales", bufs=4, align_bytes=64)
+            nc.vector.quantize_mx(out=codes[:].bitcast(E5M2), scales=scales[:], in_=tail_in[k][:])
+            tail_q[k] = (codes, scales)
+
+        def tail_mult(k):
+            mult_out1(last, k, tail_q[k][0][:], tail_q[k][1][:])
+
+        def store_out1(k, on_vector):
+            store(o1_hbm[k // 2, k % 2], acc1[k], on_vector)
+
+        store_out0(STEPS - 4, False)
+        quantize_chan(STEPS - 2)
+        turn_dz(STEPS - 1)
+        mult_out0(STEPS - 3, "dy_ps", 2)
+        tail_interleave(0)
+        mult_out0(STEPS - 2)
+        store_out0(STEPS - 3, False)
+        quantize_chan(STEPS - 1)
+        tail_quantize(0)
+        tail_interleave(1)
+        mult_out0(STEPS - 1, "dy_ps", 2)
+        tail_mult(0)
+        store_out0(STEPS - 2, False)
+        tail_interleave(2)
+        tail_quantize(1)
+        tail_mult(1)
+        store_out0(STEPS - 1, False)
+        tail_interleave(3)
+        tail_quantize(2)
+        tail_mult(2)
+        store_out1(0, False)
+        tail_quantize(3)
+        tail_mult(3)
+        store_out1(1, True)
+        store_out1(2, False)
+        store_out1(3, True)

@@ -23,6 +23,28 @@ FLOPS = 2 * 2 * N * T * C * E
 BYTES = N * T * C * 2 + N * T * 2 + E * C * 2 + N * E * T * 4 + 2 * N * E * 4 + N * E * T * 2 + N * T * C * 4 + E * C * 4
 
 
+RG_BUFS = 9
+LOADS = "r g00 m y00 k g01 y01 g02 y02 g03 y03 g10 y10 g11 w y11 g12 h0 y12 g13 y13 h1"
+W_EARLY = False
+SU = [False,True,False]
+ROUNDS = STEPS // 2 - 1
+SHORT_FROM = 99
+RG_TO = lambda r: r + 1
+EV = lambda e: False
+VEC_PLAN = {0: [("gw",0), ("u", (1, 0, True, 0, 2)), ("st", (1, 1)), ("qw",0), ("ln", (1, 1))],
+1: [("gh",0), ("u", (1, 1, True, 0, 2)), ("st", (1, 2)), ("qh",0), ("ln", (1, 2))],
+2: [("u", (1, 2, False, 0, 2)), ("gd",0), ("st", (1, 3)), ("qd",0), ("ln", (1, 3))],
+3: [("u", (1, 3, False, 0, 2)), ("gh",1), ("st", (2, 0)), ("qh",1), ("ln", (2, 0))],
+4: [("u", (2, 0, False, 0, 2)), ("gd",1), ("st", (2, 1)), ("qd",1), ("ln", (2, 1))],
+5: [("u", (2, 1, False, 0, 2)), ("gh",2), ("st", (2, 2)), ("qh",2), ("ln", (2, 2))],
+6: [("u", (2, 2, False, 0, 2)), ("gd",2), ("st", (2, 3)), ("qd",2), ("ln", (2, 3))],
+7: [("gh",3), ("u", (2, 3, False, 0, 2)), ("qh",3)],
+8: [("gd",3), ("gh",4), ("qd",3)],
+9: [("gh",5), ("qh",4), ("qh",5)],
+10: [("gd",4), ("qd",4)]}
+OUT1_AT = {r: [((r - 3) // 2, 2 * ((r - 3) % 2) + k) for k in range(2)] for r in range(3, 12)}
+
+
 def tile_transformerencoderblock_pa_v_kernel(tc, h_attn, x, masks, Wo, bo, y, mean, rstd, grad_out, out_0, out_1):
     nc = tc.nc
     with ExitStack() as ctx:
@@ -40,13 +62,19 @@ def tile_transformerencoderblock_pa_v_kernel(tc, h_attn, x, masks, Wo, bo, y, me
         g_sb, y_sb, h_sb = {}, {}, {}
         rg, uu, s_gy, s_rg, coef, shift = {}, {}, {}, {}, {}, {}
         dz_rows, chan, chan_q, tok_q, h_q, acc0 = {}, {}, {}, {}, {}, {}
-        grouped = {}
+        grouped, dz_bank = {}, {}
 
-        def load_unit(n, j):
+        def load_g(n, j):
             g_sb[n, j] = work.tile([P, T], BF16, name="g_sb", bufs=8, align_bytes=256)
             nc.sync.dma_start(out=g_sb[n, j][:], in_=g_hbm[n, j])
+
+        def load_y(n, j):
             y_sb[n, j] = work.tile([P, T], F32, name="y_sb", bufs=8, align_bytes=256)
             nc.sync.dma_start(out=y_sb[n, j][:], in_=y_hbm[n, j])
+
+        def load_unit(n, j):
+            load_g(n, j)
+            load_y(n, j)
 
         def load_h(ps):
             h_sb[ps] = work.tile([P, PACK * C], BF16, name="h_sb", bufs=3, align_bytes=256)
@@ -59,43 +87,46 @@ def tile_transformerencoderblock_pa_v_kernel(tc, h_attn, x, masks, Wo, bo, y, me
         def slot_major(ap):
             return ap.rearrange("p (s a i) -> p s a i", s=PACK, i=RUN)
 
-        load_unit(0, 0)
-        mean_sb = const.tile([P, N, PACK], F32, name="mean_sb")
-        nc.sync.dma_start(out=mean_sb[:], in_=mean.rearrange("n (p j) o -> p n (j o)", j=PACK))
         rstd_sb = const.tile([P, N, PACK], F32, name="rstd_sb")
-        nc.sync.dma_start(out=rstd_sb[:], in_=rstd.rearrange("n (p j) o -> p n (j o)", j=PACK))
-        load_unit(0, 1)
+        mean_sb = const.tile([P, N, PACK], F32, name="mean_sb")
         mask_rows = const.tile([PASSES, KP], BF16, name="mask_rows")
-        nc.sync.dma_start(out=mask_rows[:], in_=masks.rearrange("n o (g t) -> (n o g) t", g=2))
-        load_unit(0, 2)
-        load_unit(0, 3)
-        load_unit(1, 0)
         w_sb = work.tile([P, PACK * C], BF16, name="h_sb", bufs=3, align_bytes=256)
-        nc.sync.dma_start(out=w_sb[:], in_=Wo.rearrange("(p j) c -> p (j c)", j=PACK))
-        load_unit(1, 1)
-        load_h(0)
-        load_unit(1, 2)
-        load_unit(1, 3)
-        load_h(1)
+        for item in LOADS.split():
+            if item == "r":
+                nc.sync.dma_start(out=rstd_sb[:], in_=rstd.rearrange("n (p j) o -> p n (j o)", j=PACK))
+            elif item == "m":
+                nc.sync.dma_start(out=mean_sb[:], in_=mean.rearrange("n (p j) o -> p n (j o)", j=PACK))
+            elif item == "k":
+                nc.sync.dma_start(out=mask_rows[:], in_=masks.rearrange("n o (g t) -> (n o g) t", g=2))
+            elif item == "w":
+                nc.sync.dma_start(out=w_sb[:], in_=Wo.rearrange("(p j) c -> p (j c)", j=PACK))
+            elif item[0] == "h":
+                load_h(int(item[1]))
+            elif item[0] == "g":
+                load_g(int(item[1]), int(item[2]))
+            else:
+                load_y(int(item[1]), int(item[2]))
 
         ident = const.tile([P, P], F32, name="ident")
         make_identity(nc, ident[:])
         mask_pad = const.tile([P, KP], F32, name="mask_pad")
         nc.gpsimd.memset(mask_pad[:], 0.0)
+        g_term = const.tile([P, N * PACK, 2], F32, name="g_term")
+        nc.gpsimd.memset(g_term[:], 0.0)
 
         r2 = const.tile([P, N * PACK], F32, name="r2")
         kk = const.tile([P, N * PACK, 2], F32, name="kk")
         rs = rstd_sb[:].rearrange("p n j -> p (n j)")
         mn = mean_sb[:].rearrange("p n j -> p (n j)")
-        nc.vector.tensor_tensor(out=r2[:], in0=rs, in1=rs, op=ALU.mult)
-        nc.vector.scalar_tensor_tensor(out=kk[:, :, 0], in0=r2[:], scalar=-1.0 / T, in1=rs, op0=ALU.mult, op1=ALU.mult)
-        nc.vector.tensor_tensor(out=kk[:, :, 1], in0=kk[:, :, 0], in1=mn, op=ALU.mult)
 
         def scale_g(n, j):
-            rg[n, j] = work.tile([P, T], F32, name="rg", bufs=8)
+            rg[n, j] = work.tile([P, T], F32, name="rg", bufs=RG_BUFS)
             s_rg[n, j] = work.tile([P, 1], F32, name="s_rg", bufs=4)
             nc.scalar.activation(out=slot_major(rg[n, j][:]), in_=by_slot(g_sb[n, j][:]), func=ACT.Copy,
                                  scale=rstd_sb[:, n, j:j + 1], accum_out=s_rg[n, j][:])
+
+        def mean_g(n, j):
+            nc.scalar.activation(out=g_term[:, n * PACK + j, 1:2], in_=s_rg[n, j][:], func=ACT.Copy, scale=-1.0 / T)
 
         def stats(n, j):
             prod = work.tile([P, T], F32, name="prod", bufs=1)
@@ -103,22 +134,23 @@ def tile_transformerencoderblock_pa_v_kernel(tc, h_attn, x, masks, Wo, bo, y, me
             nc.vector.scalar_tensor_tensor(out=prod[:], in0=y_sb[n, j][:], scalar=mean_sb[:, n, j:j + 1], in1=g_sb[n, j][:],
                                            op0=ALU.subtract, op1=ALU.mult, accum_out=s_gy[n, j][:])
 
-        def slope(n, j):
-            coef[n, j] = work.tile([P, 2], F32, name="coef", bufs=4)
-            nc.vector.tensor_scalar(out=coef[n, j][:], in0=kk[:, n * PACK + j, :], scalar1=s_gy[n, j][:], scalar2=None, op0=ALU.mult)
+        def line(n, j):
+            coef[n, j] = work.tile([P, 2], F32, name="coef", bufs=8)
+            nc.vector.scalar_tensor_tensor(out=coef[n, j][:], in0=kk[:, n * PACK + j, :], scalar=s_gy[n, j][:],
+                                           in1=g_term[:, n * PACK + j, :], op0=ALU.mult, op1=ALU.add)
 
-        def offset(n, j):
-            shift[n, j] = work.tile([P, 1], F32, name="shift", bufs=4)
-            nc.vector.scalar_tensor_tensor(out=shift[n, j][:], in0=s_rg[n, j][:], scalar=-1.0 / T, in1=coef[n, j][:, 1:2],
-                                           op0=ALU.mult, op1=ALU.subtract)
-
-        def scale_y(n, j):
-            uu[n, j] = work.tile([P, T], F32, name="uu", bufs=8)
-            nc.vector.tensor_scalar(out=slot_major(uu[n, j][:]), in0=by_slot(y_sb[n, j][:]), scalar1=coef[n, j][:, 0:1],
-                                    scalar2=shift[n, j][:], op0=ALU.mult, op1=ALU.add)
+        def scale_y(n, j, on_scalar=False, h0=0, h1=2):
+            if h0 == 0:
+                uu[n, j] = work.tile([P, T], F32, name="uu", bufs=8)
+            dst = slot_major(uu[n, j][:])[:, :, 16 * h0:16 * h1]
+            src = by_slot(y_sb[n, j][:])[:, :, 16 * h0:16 * h1]
+            if on_scalar:
+                nc.scalar.activation(out=dst, in_=src, func=ACT.Identity, scale=coef[n, j][:, 0:1], bias=coef[n, j][:, 1:2])
+            else:
+                nc.vector.tensor_scalar(out=dst, in0=src, scalar1=coef[n, j][:, 0:1], scalar2=coef[n, j][:, 1:2], op0=ALU.mult, op1=ALU.add)
 
         def interleave(key, src):
-            grouped[key] = work.tile([P, PACK * C], BF16, name="grouped", bufs=2, align_bytes=64)
+            grouped[key] = work.tile([P, PACK * C], BF16, name="grouped", bufs=3, align_bytes=64)
             nc.vector.tensor_copy(out=grouped[key][:].rearrange("p (c i s) -> p c s i", s=PACK, i=4),
                                   in_=src[:].rearrange("p (s c i) -> p c s i", s=PACK, i=4))
 
@@ -128,70 +160,49 @@ def tile_transformerencoderblock_pa_v_kernel(tc, h_attn, x, masks, Wo, bo, y, me
             nc.vector.quantize_mx(out=codes[:].bitcast(fmt), scales=scales[:], in_=grouped[key][:])
             return codes, scales
 
-        scale_g(0, 0)
-        stats(0, 0)
-        nc.scalar.copy(out=mask_pad[0:PASSES, :].rearrange("p (s q i) -> p s q i", s=PACK, i=RUN),
-                       in_=mask_rows[:].rearrange("p (q s i) -> p s q i", s=PACK, i=RUN))
-        slope(0, 0)
-        offset(0, 0)
-        mask_ps = psum.tile([P, PACK, P], F32, name="dy_ps", bufs=2)
-        for s in range(PACK):
-            nc.tensor.transpose(mask_ps[:, s, :], mask_pad[:, s * P:(s + 1) * P], ident[:])
-        for j in range(1, PACK):
-            scale_g(0, j)
-            stats(0, j)
-            slope(0, j)
-            scale_y(0, j - 1)
-            offset(0, j)
-        mask_col = const.tile([P, PACK, PASSES], F32, name="mask_col")
-        nc.scalar.copy(out=mask_col[:], in_=mask_ps[:, :, 0:PASSES])
-        scale_y(0, PACK - 1)
-        for j in range(PACK):
-            load_unit(2, j)
-        scale_g(1, 0)
-        stats(1, 0)
-        slope(1, 0)
-
         acc1 = [psum.tile([P, C], F32, name="acc1_%d" % k) for k in range(PACK)]
         w_q = []
 
-        def turn_dy(step):
+        def turn_dy(step, u0, u1):
             ps, s = divmod(step, PACK)
             n, half = divmod(ps, 2)
-            bank = psum.tile([P, PACK, P], F32, name="dy_ps", bufs=2)
+            bank = psum.tile([P, 2 * (u1 - u0), P], F32, name="ring", bufs=4)
             cols = slice(s * 2 * P + half * P, s * 2 * P + (half + 1) * P)
-            for j in range(PACK):
-                nc.tensor.matmul(bank[:, j, :], lhsT=rg[n, j][:, cols], rhs=ident[:], start=True, stop=False, is_transpose=True)
-                nc.tensor.matmul(bank[:, j, :], lhsT=uu[n, j][:, cols], rhs=ident[:], start=False, stop=True, is_transpose=True)
+            for j in range(2 * u0, 2 * u1):
+                nc.tensor.matmul(bank[:, j - 2 * u0, :], lhsT=rg[n, j][:, cols], rhs=ident[:], start=True, stop=False, is_transpose=True)
+                nc.tensor.matmul(bank[:, j - 2 * u0, :], lhsT=uu[n, j][:, cols], rhs=ident[:], start=False, stop=True, is_transpose=True)
             return bank
 
-        def round_dz(step, bank):
+        def round_dz(step, bank, u0, u1):
             ps, s = divmod(step, PACK)
-            if s == 0:
-                dz_rows[ps] = work.tile([P, PACK * E], BF16, name="dz_rows", bufs=2, align_bytes=64)
-            nc.scalar.activation(out=dz_rows[ps][:, s * E:(s + 1) * E].rearrange("p (u m e) -> p u m e", u=2, e=2),
-                                 in_=bank[:].rearrange("p (u e) m -> p u m e", u=2), func=ACT.Copy,
+            if ps not in dz_rows:
+                dz_rows[ps] = work.tile([P, PACK * E], BF16, name="dz_rows", bufs=4, align_bytes=64)
+            nc.scalar.activation(out=dz_rows[ps][:, s * E + u0 * 2 * P:s * E + u1 * 2 * P].rearrange("p (u m e) -> p u m e", m=P, e=2),
+                                 in_=bank[:].rearrange("p (u e) m -> p u m e", e=2), func=ACT.Copy,
                                  scale=mask_col[:, s, ps:ps + 1])
 
-        def turn_dz(step):
+        def turn_dz(step, count):
             ps, s = divmod(step, PACK)
-            words = dz_rows[ps][:, s * E:(s + 1) * E].bitcast(F32)
-            bank = psum.tile([P, 2, P], F32, name="dz_ps")
-            for u in range(2):
-                nc.tensor.transpose(bank[:, u, :], words[:, u * P:(u + 1) * P], ident[:])
-            chan[step] = work.tile([P, E], BF16, name="chan", bufs=3, align_bytes=64)
-            nc.scalar.copy(out=chan[step][:].bitcast(F32).rearrange("p (t u) -> p t u", u=2), in_=bank[:].rearrange("p u t -> p t u"))
+            words = dz_rows[ps][:, s * E:(s + count) * E].bitcast(F32)
+            dz_bank[step] = psum.tile([P, count, 2, P], F32, name="ring", bufs=4)
+            for b in range(2 * count):
+                nc.tensor.transpose(dz_bank[step][:, b // 2, b % 2, :], words[:, b * P:(b + 1) * P], ident[:])
 
-        def quantize_chan(step):
-            codes = work.tile([P, P], U32, name="chan_codes", bufs=3, align_bytes=64)
-            scales = work.tile([P, P], U8, name="chan_scales", bufs=3, align_bytes=64)
+        def gather_dz(step, count):
+            chan[step] = work.tile([P, count * E], BF16, name="chan", bufs=3, align_bytes=64)
+            nc.scalar.copy(out=chan[step][:].bitcast(F32).rearrange("p (s t u) -> p s t u", u=2, t=P), in_=dz_bank[step][:].rearrange("p s u t -> p s t u"))
+
+        def quantize_chan(step, count):
+            codes = work.tile([P, count * P], U32, name="chan_codes", bufs=3, align_bytes=64)
+            scales = work.tile([P, count * P], U8, name="chan_scales", bufs=3, align_bytes=64)
             nc.vector.quantize_mx(out=codes[:].bitcast(E5M2), scales=scales[:], in_=chan[step][:])
-            chan_q[step] = (codes, scales)
+            for b in range(count):
+                chan_q[step + b] = (codes[:, b * P:(b + 1) * P], scales[:, b * P:(b + 1) * P])
 
-        def mult_out0(step, name="acc0", bufs=1):
+        def mult_out0(step):
             codes, scales = chan_q[step]
-            acc0[step] = psum.tile([P, C], F32, name=name, bufs=bufs)
-            nc.tensor.matmul_mx(out=acc0[step][:], lhsT=codes[:].bitcast(E5M2), lhsT_scale=scales[:],
+            acc0[step] = psum.tile([P, C], F32, name="ring", bufs=4)
+            nc.tensor.matmul_mx(out=acc0[step][:], lhsT=codes.bitcast(E5M2), lhsT_scale=scales,
                                 rhs=w_q[0][:].bitcast(E4M3), rhs_scale=w_q[1][:], start=True, stop=True)
 
         def mult_out1(ps, k, codes, scales):
@@ -214,63 +225,130 @@ def tile_transformerencoderblock_pa_v_kernel(tc, h_attn, x, masks, Wo, bo, y, me
             ps, s = divmod(step, PACK)
             store(o0_hbm[ps // 2, ps % 2, s], acc0[step], on_vector)
 
-        for step in range(STEPS):
-            ps, s = divmod(step, PACK)
-            nxt = (step + 1) // (2 * PACK) + 1
-            j = ((step + 1) % (2 * PACK)) // 2
-            last_phase = step >= STEPS - 2 * PACK
-            if step >= 4 and not (last_phase and step % 2 == 1):
-                store_out0(step - 4, False)
-            bank = turn_dy(step)
-            if step % 2 == 1 and nxt < N:
-                scale_g(nxt, j)
-            round_dz(step, bank)
-            if step >= 1:
-                turn_dz(step - 1)
-            if step >= 4 and last_phase and step % 2 == 1:
-                store_out0(step - 4, True)
-            if step >= 2:
-                quantize_chan(step - 2)
-            if nxt < N:
-                if step % 2 == 1:
-                    stats(nxt, j)
-                else:
-                    offset(nxt, j)
-            if s == 0:
-                if ps == 0:
-                    interleave("w", w_sb)
-                else:
-                    interleave(("dz", ps - 1), dz_rows[ps - 1])
-            elif s == 1:
-                if ps == 0:
-                    w_q.extend(quantize("w", "w", E4M3, 1))
-                else:
-                    tok_q[ps - 1] = quantize(("dz", ps - 1), "tok", E5M2, 2)
-            elif s == 2:
-                interleave(("h", ps), h_sb[ps])
-                if ps + 2 < PASSES:
-                    load_h(ps + 2)
+        def group_h(ps):
+            interleave(("h", ps), h_sb[ps])
+            if ps + 2 < PASSES:
+                load_h(ps + 2)
+
+        def quantize_h(ps):
+            h_q[ps] = quantize(("h", ps), "h", E4M3, 3)
+
+        def group_dz(ps):
+            interleave(("dz", ps), dz_rows[ps])
+
+        def quantize_dz(ps):
+            tok_q[ps] = quantize(("dz", ps), "tok", E5M2, 2)
+
+        nc.vector.tensor_tensor(out=r2[:], in0=rs, in1=rs, op=ALU.mult)
+        nc.vector.scalar_tensor_tensor(out=kk[:, :, 0], in0=r2[:], scalar=-1.0 / T, in1=rs, op0=ALU.mult, op1=ALU.mult)
+        nc.vector.scalar_tensor_tensor(out=kk[:, :, 1], in0=kk[:, :, 0], scalar=-1.0, in1=mn, op0=ALU.mult, op1=ALU.mult)
+        scale_g(0, 0)
+        stats(0, 0)
+        nc.scalar.copy(out=mask_pad[0:PASSES, :].rearrange("p (s q i) -> p s q i", s=PACK, i=RUN),
+                       in_=mask_rows[:].rearrange("p (q s i) -> p s q i", s=PACK, i=RUN))
+        mean_g(0, 0)
+        line(0, 0)
+        mask_ps = psum.tile([P, PACK, P], F32, name="ring", bufs=4)
+        for s in range(PACK):
+            nc.tensor.transpose(mask_ps[:, s, :], mask_pad[:, s * P:(s + 1) * P], ident[:])
+        mask_col = const.tile([P, PACK, PASSES], F32, name="mask_col")
+        scale_g(0, 1)
+        nc.scalar.copy(out=mask_col[:], in_=mask_ps[:, :, 0:PASSES])
+        mean_g(0, 1)
+        stats(0, 1)
+        scale_y(0, 0, SU[0])
+        line(0, 1)
+        if W_EARLY:
+            interleave("w", w_sb)
+        scale_g(0, 2)
+        scale_y(0, 1, SU[1])
+        mean_g(0, 2)
+        stats(0, 2)
+        if W_EARLY:
+            w_q.extend(quantize("w", "w", E4M3, 1))
+        scale_g(0, 3)
+        line(0, 2)
+        mean_g(0, 3)
+        stats(0, 3)
+        scale_y(0, 2, SU[2])
+        line(0, 3)
+        scale_g(1, 0)
+        scale_y(0, 3)
+        stats(1, 0)
+        for j in range(PACK):
+            load_unit(2, j)
+
+        units = [(n, j) for n in range(1, N) for j in range(PACK)]
+        last = PASSES - 1
+        nrg = 1
+        nq = 0
+        for r in range(ROUNDS):
+            a, b = 2 * r, 2 * r + 1
+            short = r >= SHORT_FROM
+            if short:
+                turn_dz(a - 2, 2)
+                gather_dz(a - 2, 2)
+            bank_a = turn_dy(a, 0, 2)
+            bank_b = turn_dy(b, 0, 2)
+            if r == 0:
+                mean_g(*units[0])
+                line(*units[0])
+            todo = []
+            while nrg < len(units) and nrg <= RG_TO(r):
+                todo.append(units[nrg])
+                nrg = nrg + 1
+            for un in todo[:1]:
+                scale_g(*un)
+            round_dz(a, bank_a, 0, 2)
+            for un in todo[:1]:
+                mean_g(*un)
+            for un in todo[1:]:
+                scale_g(*un)
+            round_dz(b, bank_b, 0, 2)
+            for un in todo[1:]:
+                mean_g(*un)
+            if r >= 1 and not short:
+                turn_dz(a - 2, 2)
+                gather_dz(a - 2, 2)
+            pairs = []
+            if r >= 2 and r <= SHORT_FROM:
+                quantize_chan(a - 4, 2)
+                pairs.append(a - 4)
+            for (what, arg) in VEC_PLAN.get(r, []):
+                if what == "qc":
+                    quantize_chan(a - 2, 2)
+                    pairs.append(a - 2)
+                    continue
+                {"st": lambda a: stats(*a), "ln": lambda a: line(*a), "u": lambda a: scale_y(*a), "gh": group_h, "qh": quantize_h,
+                 "gd": group_dz, "qd": quantize_dz, "gw": lambda a: interleave("w", w_sb), "qw": lambda a: w_q.extend(quantize("w", "w", E4M3, 1))}[what](arg)
+            if not short:
+                if r >= 2:
+                    mult_out0(a - 4)
+                for (p1, k) in OUT1_AT.get(r, []):
+                    mult_out1_tile(p1, k)
+                if r >= 2:
+                    mult_out0(a - 3)
+                    store_out0(a - 4, False)
+                    store_out0(a - 3, False)
             else:
-                h_q[ps] = quantize(("h", ps), "h", E4M3, 2)
-            if nxt < N:
-                if step % 2 == 1:
-                    slope(nxt, j)
-                else:
-                    scale_y(nxt, j)
-            if step >= 3:
-                mult_out0(step - 3)
-            if step >= 6 and step < STEPS - 2:
-                mult_out1_tile((step - 6) // PACK, (step - 6) % PACK)
-            elif step >= STEPS - 2:
-                for k in range(2):
-                    mult_out1_tile(PASSES - 2, 2 * (step - STEPS + 2) + k)
+                if len(pairs) == 2:
+                    mult_out0(pairs[0])
+                    store_out0(pairs[0], False)
+                    mult_out0(pairs[0] + 1)
+                    store_out0(pairs[0] + 1, False)
+                for (p1, k) in OUT1_AT.get(r, []):
+                    mult_out1_tile(p1, k)
+                mult_out0(a - 2)
+                mult_out0(a - 1)
+                store_out0(a - 2, False)
+                store_out0(a - 1, EV(r))
 
         last = PASSES - 1
         tail_in = {}
         tail_q = {}
 
         def tail_interleave(k):
-            tail_in[k] = work.tile([P, PACK * P], BF16, name="chan", bufs=3, align_bytes=64)
+            tail_in[k] = work.tile([P, PACK * P], BF16, name="tail_in", bufs=2, align_bytes=64)
             nc.vector.tensor_copy(out=tail_in[k][:].rearrange("p (c i s) -> p c s i", s=PACK, i=4),
                                   in_=dz_rows[last][:].rearrange("p (s c i) -> p c s i", s=PACK, i=4)[:, k * 32:(k + 1) * 32])
 
@@ -286,29 +364,47 @@ def tile_transformerencoderblock_pa_v_kernel(tc, h_attn, x, masks, Wo, bo, y, me
         def store_out1(k, on_vector):
             store(o1_hbm[k // 2, k % 2], acc1[k], on_vector)
 
-        store_out0(STEPS - 4, False)
-        quantize_chan(STEPS - 2)
-        turn_dz(STEPS - 1)
-        mult_out0(STEPS - 3, "dy_ps", 2)
+        e = STEPS
+        turn_dz(e - 4, 2)
+        gather_dz(e - 4, 2)
+        bank_a = turn_dy(e - 2, 0, 2)
+        bank_b = turn_dy(e - 1, 0, 2)
+        round_dz(e - 2, bank_a, 0, 2)
+        round_dz(e - 1, bank_b, 0, 2)
+        quantize_chan(e - 6, 2)
+        quantize_chan(e - 4, 2)
+        mult_out0(e - 6)
+        mult_out0(e - 5)
+        mult_out0(e - 4)
+        store_out0(e - 6, True)
+        store_out0(e - 4, False)
+        turn_dz(e - 2, 2)
+        gather_dz(e - 2, 2)
+        mult_out0(e - 3)
         tail_interleave(0)
-        mult_out0(STEPS - 2)
-        store_out0(STEPS - 3, False)
-        quantize_chan(STEPS - 1)
+        store_out0(e - 5, True)
         tail_quantize(0)
         tail_interleave(1)
-        mult_out0(STEPS - 1, "dy_ps", 2)
+        mult_out1_tile(last - 1, 0)
         tail_mult(0)
-        store_out0(STEPS - 2, False)
-        tail_interleave(2)
+        mult_out1_tile(last - 1, 1)
+        store_out0(e - 3, False)
         tail_quantize(1)
+        quantize_chan(e - 2, 2)
+        store_out1(0, False)
         tail_mult(1)
-        store_out0(STEPS - 1, False)
+        mult_out1_tile(last - 1, 2)
+        mult_out0(e - 2)
+        mult_out0(e - 1)
+        mult_out1_tile(last - 1, 3)
+        tail_interleave(2)
         tail_interleave(3)
         tail_quantize(2)
-        tail_mult(2)
-        store_out1(0, False)
         tail_quantize(3)
+        tail_mult(2)
         tail_mult(3)
-        store_out1(1, True)
+        store_out1(1, False)
+        store_out0(e - 2, False)
+        store_out0(e - 1, True)
         store_out1(2, False)
         store_out1(3, True)

from contextlib import ExitStack

import concourse.mybir as mybir
from concourse.masks import make_identity

F32 = mybir.dt.float32
BF16 = mybir.dt.bfloat16
U32 = mybir.dt.uint32
U8 = mybir.dt.uint8
E4M3 = mybir.dt.float8_e4m3fn_x4
E5M2 = mybir.dt.float8_e5m2_x4
ALU = mybir.AluOpType
ACT = mybir.ActivationFunctionType

N, T, C, E = 3, 1024, 512, 512
P = 128
PACK = 4
KP = P * PACK
PASSES = N * T // KP
STEPS = PASSES * PACK
RUN = 8
FLOPS = 2 * 2 * N * T * C * E
BYTES = N * T * C * 2 + N * T * 2 + E * C * 2 + N * E * T * 4 + 2 * N * E * 4 + N * E * T * 2 + N * T * C * 4 + E * C * 4


RG_BUFS = 9
LOADS = "r g00 m y00 k g01 y01 g02 y02 g03 y03 g10 y10 g11 w y11 g12 h0 y12 g13 y13 h1"
W_EARLY = False
SU = [False,True,False]
ROUNDS = STEPS // 2 - 1
SHORT_FROM = 99
RG_TO = lambda r: r + 1
EV = lambda e: False
VEC_PLAN = {0: [("gw",0), ("u", (1, 0, True, 0, 2)), ("st", (1, 1)), ("qw",0), ("ln", (1, 1))],
1: [("gh",0), ("u", (1, 1, True, 0, 2)), ("st", (1, 2)), ("qh",0), ("ln", (1, 2))],
2: [("u", (1, 2, False, 0, 2)), ("gd",0), ("st", (1, 3)), ("qd",0), ("ln", (1, 3))],
3: [("u", (1, 3, False, 0, 2)), ("gh",1), ("st", (2, 0)), ("qh",1), ("ln", (2, 0))],
4: [("u", (2, 0, False, 0, 2)), ("gd",1), ("st", (2, 1)), ("qd",1), ("ln", (2, 1))],
5: [("u", (2, 1, False, 0, 2)), ("gh",2), ("st", (2, 2)), ("qh",2), ("ln", (2, 2))],
6: [("u", (2, 2, False, 0, 2)), ("gd",2), ("st", (2, 3)), ("qd",2), ("ln", (2, 3))],
7: [("gh",3), ("u", (2, 3, False, 0, 2)), ("qh",3)],
8: [("gd",3), ("gh",4), ("qd",3)],
9: [("gh",5), ("qh",4), ("qh",5)],
10: [("gd",4), ("qd",4)]}
OUT1_AT = {r: [((r - 3) // 2, 2 * ((r - 3) % 2) + k) for k in range(2)] for r in range(3, 12)}


def tile_transformerencoderblock_pa_v_kernel(tc, h_attn, x, masks, Wo, bo, y, mean, rstd, grad_out, out_0, out_1):
    nc = tc.nc
    with ExitStack() as ctx:
        const = ctx.enter_context(tc.tile_pool(name="const", bufs=1))
        work = ctx.enter_context(tc.tile_pool(name="work", bufs=2))
        psum = ctx.enter_context(tc.psum_pool(name="psum", bufs=1))
        ctx.enter_context(tc.manual_schedule())

        g_hbm = grad_out.rearrange("n (p j) t -> n j p t", j=PACK)
        y_hbm = y.rearrange("n (p j) t -> n j p t", j=PACK)
        h_hbm = h_attn.rearrange("n (g q s i) c -> n g s q i c", g=2, s=PACK, i=RUN)
        o0_hbm = out_0.rearrange("n (g q s i) c -> n g s q i c", g=2, s=PACK, i=RUN)
        o1_hbm = out_1.rearrange("(a m u e) c -> u a m e c", a=2, u=2, e=2)

        g_sb, y_sb, h_sb = {}, {}, {}
        rg, uu, s_gy, s_rg, coef, shift = {}, {}, {}, {}, {}, {}
        dz_rows, chan, chan_q, tok_q, h_q, acc0 = {}, {}, {}, {}, {}, {}
        grouped, dz_bank = {}, {}

        def load_g(n, j):
            g_sb[n, j] = work.tile([P, T], BF16, name="g_sb", bufs=8, align_bytes=256)
            nc.sync.dma_start(out=g_sb[n, j][:], in_=g_hbm[n, j])

        def load_y(n, j):
            y_sb[n, j] = work.tile([P, T], F32, name="y_sb", bufs=8, align_bytes=256)
            nc.sync.dma_start(out=y_sb[n, j][:], in_=y_hbm[n, j])

        def load_unit(n, j):
            load_g(n, j)
            load_y(n, j)

        def load_h(ps):
            h_sb[ps] = work.tile([P, PACK * C], BF16, name="h_sb", bufs=3, align_bytes=256)
            for s in range(PACK):
                nc.sync.dma_start(out=h_sb[ps][:, s * C:(s + 1) * C], in_=h_hbm[ps // 2, ps % 2, s])

        def by_slot(ap):
            return ap.rearrange("p (a s i) -> p s a i", s=PACK, i=RUN)

        def slot_major(ap):
            return ap.rearrange("p (s a i) -> p s a i", s=PACK, i=RUN)

        rstd_sb = const.tile([P, N, PACK], F32, name="rstd_sb")
        mean_sb = const.tile([P, N, PACK], F32, name="mean_sb")
        mask_rows = const.tile([PASSES, KP], BF16, name="mask_rows")
        w_sb = work.tile([P, PACK * C], BF16, name="h_sb", bufs=3, align_bytes=256)
        for item in LOADS.split():
            if item == "r":
                nc.sync.dma_start(out=rstd_sb[:], in_=rstd.rearrange("n (p j) o -> p n (j o)", j=PACK))
            elif item == "m":
                nc.sync.dma_start(out=mean_sb[:], in_=mean.rearrange("n (p j) o -> p n (j o)", j=PACK))
            elif item == "k":
                nc.sync.dma_start(out=mask_rows[:], in_=masks.rearrange("n o (g t) -> (n o g) t", g=2))
            elif item == "w":
                nc.sync.dma_start(out=w_sb[:], in_=Wo.rearrange("(p j) c -> p (j c)", j=PACK))
            elif item[0] == "h":
                load_h(int(item[1]))
            elif item[0] == "g":
                load_g(int(item[1]), int(item[2]))
            else:
                load_y(int(item[1]), int(item[2]))

        ident = const.tile([P, P], F32, name="ident")
        make_identity(nc, ident[:])
        mask_pad = const.tile([P, KP], F32, name="mask_pad")
        nc.gpsimd.memset(mask_pad[:], 0.0)
        g_term = const.tile([P, N * PACK, 2], F32, name="g_term")
        nc.gpsimd.memset(g_term[:], 0.0)

        r2 = const.tile([P, N * PACK], F32, name="r2")
        kk = const.tile([P, N * PACK, 2], F32, name="kk")
        rs = rstd_sb[:].rearrange("p n j -> p (n j)")
        mn = mean_sb[:].rearrange("p n j -> p (n j)")

        def scale_g(n, j):
            rg[n, j] = work.tile([P, T], F32, name="rg", bufs=RG_BUFS)
            s_rg[n, j] = work.tile([P, 1], F32, name="s_rg", bufs=4)
            nc.scalar.activation(out=slot_major(rg[n, j][:]), in_=by_slot(g_sb[n, j][:]), func=ACT.Copy,
                                 scale=rstd_sb[:, n, j:j + 1], accum_out=s_rg[n, j][:])

        def mean_g(n, j):
            nc.scalar.activation(out=g_term[:, n * PACK + j, 1:2], in_=s_rg[n, j][:], func=ACT.Copy, scale=-1.0 / T)

        def stats(n, j):
            prod = work.tile([P, T], F32, name="prod", bufs=1)
            s_gy[n, j] = work.tile([P, 1], F32, name="s_gy", bufs=4)
            nc.vector.scalar_tensor_tensor(out=prod[:], in0=y_sb[n, j][:], scalar=mean_sb[:, n, j:j + 1], in1=g_sb[n, j][:],
                                           op0=ALU.subtract, op1=ALU.mult, accum_out=s_gy[n, j][:])

        def line(n, j):
            coef[n, j] = work.tile([P, 2], F32, name="coef", bufs=8)
            nc.vector.scalar_tensor_tensor(out=coef[n, j][:], in0=kk[:, n * PACK + j, :], scalar=s_gy[n, j][:],
                                           in1=g_term[:, n * PACK + j, :], op0=ALU.mult, op1=ALU.add)

        def scale_y(n, j, on_scalar=False, h0=0, h1=2):
            if h0 == 0:
                uu[n, j] = work.tile([P, T], F32, name="uu", bufs=8)
            dst = slot_major(uu[n, j][:])[:, :, 16 * h0:16 * h1]
            src = by_slot(y_sb[n, j][:])[:, :, 16 * h0:16 * h1]
            if on_scalar:
                nc.scalar.activation(out=dst, in_=src, func=ACT.Identity, scale=coef[n, j][:, 0:1], bias=coef[n, j][:, 1:2])
            else:
                nc.vector.tensor_scalar(out=dst, in0=src, scalar1=coef[n, j][:, 0:1], scalar2=coef[n, j][:, 1:2], op0=ALU.mult, op1=ALU.add)

        def interleave(key, src):
            grouped[key] = work.tile([P, PACK * C], BF16, name="grouped", bufs=3, align_bytes=64)
            nc.vector.tensor_copy(out=grouped[key][:].rearrange("p (c i s) -> p c s i", s=PACK, i=4),
                                  in_=src[:].rearrange("p (s c i) -> p c s i", s=PACK, i=4))

        def quantize(key, name, fmt, bufs):
            codes = work.tile([P, C], U32, name=name + "_codes", bufs=bufs, align_bytes=64)
            scales = work.tile([P, C], U8, name=name + "_scales", bufs=bufs, align_bytes=64)
            nc.vector.quantize_mx(out=codes[:].bitcast(fmt), scales=scales[:], in_=grouped[key][:])
            return codes, scales

        acc1 = [psum.tile([P, C], F32, name="acc1_%d" % k) for k in range(PACK)]
        w_q = []

        def turn_dy(step, u0, u1):
            ps, s = divmod(step, PACK)
            n, half = divmod(ps, 2)
            bank = psum.tile([P, 2 * (u1 - u0), P], F32, name="ring", bufs=4)
            cols = slice(s * 2 * P + half * P, s * 2 * P + (half + 1) * P)
            for j in range(2 * u0, 2 * u1):
                nc.tensor.matmul(bank[:, j - 2 * u0, :], lhsT=rg[n, j][:, cols], rhs=ident[:], start=True, stop=False, is_transpose=True)
                nc.tensor.matmul(bank[:, j - 2 * u0, :], lhsT=uu[n, j][:, cols], rhs=ident[:], start=False, stop=True, is_transpose=True)
            return bank

        def round_dz(step, bank, u0, u1):
            ps, s = divmod(step, PACK)
            if ps not in dz_rows:
                dz_rows[ps] = work.tile([P, PACK * E], BF16, name="dz_rows", bufs=4, align_bytes=64)
            nc.scalar.activation(out=dz_rows[ps][:, s * E + u0 * 2 * P:s * E + u1 * 2 * P].rearrange("p (u m e) -> p u m e", m=P, e=2),
                                 in_=bank[:].rearrange("p (u e) m -> p u m e", e=2), func=ACT.Copy,
                                 scale=mask_col[:, s, ps:ps + 1])

        def turn_dz(step, count):
            ps, s = divmod(step, PACK)
            words = dz_rows[ps][:, s * E:(s + count) * E].bitcast(F32)
            dz_bank[step] = psum.tile([P, count, 2, P], F32, name="ring", bufs=4)
            for b in range(2 * count):
                nc.tensor.transpose(dz_bank[step][:, b // 2, b % 2, :], words[:, b * P:(b + 1) * P], ident[:])

        def gather_dz(step, count):
            chan[step] = work.tile([P, count * E], BF16, name="chan", bufs=3, align_bytes=64)
            nc.scalar.copy(out=chan[step][:].bitcast(F32).rearrange("p (s t u) -> p s t u", u=2, t=P), in_=dz_bank[step][:].rearrange("p s u t -> p s t u"))

        def quantize_chan(step, count):
            codes = work.tile([P, count * P], U32, name="chan_codes", bufs=3, align_bytes=64)
            scales = work.tile([P, count * P], U8, name="chan_scales", bufs=3, align_bytes=64)
            nc.vector.quantize_mx(out=codes[:].bitcast(E5M2), scales=scales[:], in_=chan[step][:])
            for b in range(count):
                chan_q[step + b] = (codes[:, b * P:(b + 1) * P], scales[:, b * P:(b + 1) * P])

        def mult_out0(step):
            codes, scales = chan_q[step]
            acc0[step] = psum.tile([P, C], F32, name="ring", bufs=4)
            nc.tensor.matmul_mx(out=acc0[step][:], lhsT=codes.bitcast(E5M2), lhsT_scale=scales,
                                rhs=w_q[0][:].bitcast(E4M3), rhs_scale=w_q[1][:], start=True, stop=True)

        def mult_out1(ps, k, codes, scales):
            nc.tensor.matmul_mx(out=acc1[k][:], lhsT=codes.bitcast(E5M2), lhsT_scale=scales,
                                rhs=h_q[ps][0][:].bitcast(E4M3), rhs_scale=h_q[ps][1][:], start=(ps == 0), stop=(ps == PASSES - 1))

        def mult_out1_tile(ps, k):
            codes, scales = tok_q[ps]
            mult_out1(ps, k, codes[:, k * P:(k + 1) * P], scales[:, k * P:(k + 1) * P])

        def store(dst, acc, on_vector):
            res = work.tile([P, C], F32, name="res", bufs=8, align_bytes=256)
            if on_vector:
                nc.vector.tensor_copy(out=res[:], in_=acc[:])
            else:
                nc.scalar.copy(out=res[:], in_=acc[:])
            nc.sync.dma_start(out=dst, in_=res[:])

        def store_out0(step, on_vector):
            ps, s = divmod(step, PACK)
            store(o0_hbm[ps // 2, ps % 2, s], acc0[step], on_vector)

        def group_h(ps):
            interleave(("h", ps), h_sb[ps])
            if ps + 2 < PASSES:
                load_h(ps + 2)

        def quantize_h(ps):
            h_q[ps] = quantize(("h", ps), "h", E4M3, 3)

        def group_dz(ps):
            interleave(("dz", ps), dz_rows[ps])

        def quantize_dz(ps):
            tok_q[ps] = quantize(("dz", ps), "tok", E5M2, 2)

        nc.vector.tensor_tensor(out=r2[:], in0=rs, in1=rs, op=ALU.mult)
        nc.vector.scalar_tensor_tensor(out=kk[:, :, 0], in0=r2[:], scalar=-1.0 / T, in1=rs, op0=ALU.mult, op1=ALU.mult)
        nc.vector.scalar_tensor_tensor(out=kk[:, :, 1], in0=kk[:, :, 0], scalar=-1.0, in1=mn, op0=ALU.mult, op1=ALU.mult)
        scale_g(0, 0)
        stats(0, 0)
        nc.scalar.copy(out=mask_pad[0:PASSES, :].rearrange("p (s q i) -> p s q i", s=PACK, i=RUN),
                       in_=mask_rows[:].rearrange("p (q s i) -> p s q i", s=PACK, i=RUN))
        mean_g(0, 0)
        line(0, 0)
        mask_ps = psum.tile([P, PACK, P], F32, name="ring", bufs=4)
        for s in range(PACK):
            nc.tensor.transpose(mask_ps[:, s, :], mask_pad[:, s * P:(s + 1) * P], ident[:])
        mask_col = const.tile([P, PACK, PASSES], F32, name="mask_col")
        scale_g(0, 1)
        nc.scalar.copy(out=mask_col[:], in_=mask_ps[:, :, 0:PASSES])
        mean_g(0, 1)
        stats(0, 1)
        scale_y(0, 0, SU[0])
        line(0, 1)
        if W_EARLY:
            interleave("w", w_sb)
        scale_g(0, 2)
        scale_y(0, 1, SU[1])
        mean_g(0, 2)
        stats(0, 2)
        if W_EARLY:
            w_q.extend(quantize("w", "w", E4M3, 1))
        scale_g(0, 3)
        line(0, 2)
        mean_g(0, 3)
        stats(0, 3)
        scale_y(0, 2, SU[2])
        line(0, 3)
        scale_g(1, 0)
        scale_y(0, 3)
        stats(1, 0)
        for j in range(PACK):
            load_unit(2, j)

        units = [(n, j) for n in range(1, N) for j in range(PACK)]
        last = PASSES - 1
        nrg = 1
        nq = 0
        for r in range(ROUNDS):
            a, b = 2 * r, 2 * r + 1
            short = r >= SHORT_FROM
            if short:
                turn_dz(a - 2, 2)
                gather_dz(a - 2, 2)
            bank_a = turn_dy(a, 0, 2)
            bank_b = turn_dy(b, 0, 2)
            if r == 0:
                mean_g(*units[0])
                line(*units[0])
            todo = []
            while nrg < len(units) and nrg <= RG_TO(r):
                todo.append(units[nrg])
                nrg = nrg + 1
            for un in todo[:1]:
                scale_g(*un)
            round_dz(a, bank_a, 0, 2)
            for un in todo[:1]:
                mean_g(*un)
            for un in todo[1:]:
                scale_g(*un)
            round_dz(b, bank_b, 0, 2)
            for un in todo[1:]:
                mean_g(*un)
            if r >= 1 and not short:
                turn_dz(a - 2, 2)
                gather_dz(a - 2, 2)
            pairs = []
            if r >= 2 and r <= SHORT_FROM:
                quantize_chan(a - 4, 2)
                pairs.append(a - 4)
            for (what, arg) in VEC_PLAN.get(r, []):
                if what == "qc":
                    quantize_chan(a - 2, 2)
                    pairs.append(a - 2)
                    continue
                {"st": lambda a: stats(*a), "ln": lambda a: line(*a), "u": lambda a: scale_y(*a), "gh": group_h, "qh": quantize_h,
                 "gd": group_dz, "qd": quantize_dz, "gw": lambda a: interleave("w", w_sb), "qw": lambda a: w_q.extend(quantize("w", "w", E4M3, 1))}[what](arg)
            if not short:
                if r >= 2:
                    mult_out0(a - 4)
                for (p1, k) in OUT1_AT.get(r, []):
                    mult_out1_tile(p1, k)
                if r >= 2:
                    mult_out0(a - 3)
                    store_out0(a - 4, False)
                    store_out0(a - 3, False)
            else:
                if len(pairs) == 2:
                    mult_out0(pairs[0])
                    store_out0(pairs[0], False)
                    mult_out0(pairs[0] + 1)
                    store_out0(pairs[0] + 1, False)
                for (p1, k) in OUT1_AT.get(r, []):
                    mult_out1_tile(p1, k)
                mult_out0(a - 2)
                mult_out0(a - 1)
                store_out0(a - 2, False)
                store_out0(a - 1, EV(r))

        last = PASSES - 1
        tail_in = {}
        tail_q = {}

        def tail_interleave(k):
            tail_in[k] = work.tile([P, PACK * P], BF16, name="tail_in", bufs=2, align_bytes=64)
            nc.vector.tensor_copy(out=tail_in[k][:].rearrange("p (c i s) -> p c s i", s=PACK, i=4),
                                  in_=dz_rows[last][:].rearrange("p (s c i) -> p c s i", s=PACK, i=4)[:, k * 32:(k + 1) * 32])

        def tail_quantize(k):
            codes = work.tile([P, P], U32, name="tail_codes", bufs=4, align_bytes=64)
            scales = work.tile([P, P], U8, name="tail_scales", bufs=4, align_bytes=64)
            nc.vector.quantize_mx(out=codes[:].bitcast(E5M2), scales=scales[:], in_=tail_in[k][:])
            tail_q[k] = (codes, scales)

        def tail_mult(k):
            mult_out1(last, k, tail_q[k][0][:], tail_q[k][1][:])

        def store_out1(k, on_vector):
            store(o1_hbm[k // 2, k % 2], acc1[k], on_vector)

        e = STEPS
        turn_dz(e - 4, 2)
        gather_dz(e - 4, 2)
        bank_a = turn_dy(e - 2, 0, 2)
        bank_b = turn_dy(e - 1, 0, 2)
        round_dz(e - 2, bank_a, 0, 2)
        round_dz(e - 1, bank_b, 0, 2)
        quantize_chan(e - 6, 2)
        quantize_chan(e - 4, 2)
        mult_out0(e - 6)
        mult_out0(e - 5)
        mult_out0(e - 4)
        store_out0(e - 6, True)
        store_out0(e - 4, False)
        turn_dz(e - 2, 2)
        gather_dz(e - 2, 2)
        mult_out0(e - 3)
        tail_interleave(0)
        store_out0(e - 5, True)
        tail_quantize(0)
        tail_interleave(1)
        mult_out1_tile(last - 1, 0)
        tail_mult(0)
        mult_out1_tile(last - 1, 1)
        store_out0(e - 3, False)
        tail_quantize(1)
        quantize_chan(e - 2, 2)
        store_out1(0, False)
        tail_mult(1)
        mult_out1_tile(last - 1, 2)
        mult_out0(e - 2)
        mult_out0(e - 1)
        mult_out1_tile(last - 1, 3)
        tail_interleave(2)
        tail_interleave(3)
        tail_quantize(2)
        tail_quantize(3)
        tail_mult(2)
        tail_mult(3)
        store_out1(1, False)
        store_out0(e - 2, False)
        store_out0(e - 1, True)
        store_out1(2, False)
        store_out1(3, True)
